import numpy as np
import ml_dtypes


def mxq(x, axis, fmt="e4m3"):
    dtype, down = {"e4m3": (ml_dtypes.float8_e4m3fn, 7), "e5m2": (ml_dtypes.float8_e5m2, 14)}[fmt]
    v = np.moveaxis(np.asarray(x, np.float32).astype(ml_dtypes.bfloat16).astype(np.float64), axis, -1)
    blocks = v.reshape(v.shape[:-1] + (-1, 32))
    amax = np.abs(blocks).max(-1, keepdims=True)
    byte = np.maximum(np.where(amax > 0, np.frexp(amax)[1] - 1 + 127, 0) - down, 1)
    scale = np.exp2(byte - 127.0)
    codes = (blocks / scale).astype(np.float32).astype(dtype).astype(np.float64)
    return np.moveaxis((codes * scale).reshape(v.shape), -1, axis)


WIDE = False


def mx_kscale(k):
    if not WIDE:
        return np.ones(k)
    levels = np.array([10, -10, 5, -5, 0])
    a = np.random.permutation(np.resize(levels, k // 512 * 4)).reshape(k // 512, 4)
    idx = np.arange(k)
    return np.exp2(a[idx // 512, idx % 128 // 32])


BF16 = ml_dtypes.bfloat16


def bf(x):
    return np.asarray(x, np.float32).astype(BF16)


def f64(x):
    return np.asarray(x).astype(np.float64)


B, T, D, F = 4, 32, 512, 256
K2, K3, K4 = 2, 3, 4
EPS = 1e-12


def conv_branch(xq, w, b):
    kw = w.shape[1]
    n = xq.shape[1] - kw + 1
    wq = mxq(f64(w), 2, "e4m3")
    out = sum((xq[:, k:k + n, :] @ wq[:, k, :].T) for k in range(kw))
    return np.maximum(out + f64(b), 0.0)


def l2norm(x, axis):
    n = np.sqrt(np.sum(x * x, axis=axis, keepdims=True))
    return x / np.maximum(n, EPS)


def setup_inputs():
    s = mx_kscale(D)
    return {"words_emb": bf(np.random.standard_normal((B, T, D)) * s),
            "W2": bf(np.random.standard_normal((F, K2, D)) / np.sqrt(K2 * D) / s), "b2": bf(np.random.standard_normal(F) * 0.3),
            "W3": bf(np.random.standard_normal((F, K3, D)) / np.sqrt(K3 * D) / s), "b3": bf(np.random.standard_normal(F) * 0.3),
            "W4": bf(np.random.standard_normal((F, K4, D)) / np.sqrt(K4 * D) / s), "b4": bf(np.random.standard_normal(F) * 0.3)}


def reference(words_emb, W2, b2, W3, b3, W4, b4):
    xq = mxq(f64(words_emb), 2, "e4m3")
    a = conv_branch(xq, W2, b2)
    b_ = conv_branch(xq, W3, b3)
    c = conv_branch(xq, W4, b4)
    seq = T - K4 + 1
    main = np.maximum(np.maximum(a[:, :seq], b_[:, :seq]), c[:, :seq])
    pen = np.maximum(a[:, seq], b_[:, seq])[:, None]
    last = a[:, seq + 1][:, None]
    code = np.concatenate([main, pen, last], axis=1)
    code = l2norm(code, 2)
    return code.transpose(0, 2, 1)

@@ -1,0 +1,174 @@
+from contextlib import ExitStack
+
+import concourse.mybir as mybir
+from concourse.masks import make_identity
+
+F32 = mybir.dt.float32
+BF16 = mybir.dt.bfloat16
+U32 = mybir.dt.uint32
+U8 = mybir.dt.uint8
+FP8X4 = mybir.dt.float8_e4m3fn_x4
+ALU = mybir.AluOpType
+ACT = mybir.ActivationFunctionType
+
+P = 128
+PACK = 4
+TEXTS, WORDS, FEATURES, FILTERS = 4, 32, 512, 256
+TOKENS = TEXTS * WORDS
+WIDTHS = (2, 3, 4)
+SHIFTS = max(WIDTHS)
+PARITIES = FILTERS // P
+POSITIONS = WORDS - min(WIDTHS) + 1
+EPS = 1e-12
+PAIRS = FEATURES // 2
+HALVES = PAIRS // P
+SLABS_PER_BANK = 2
+SLAB_COLS = P * PACK
+
+assert TOKENS == P and FEATURES == P * PACK
+
+FLOPS = 2 * FEATURES * FILTERS * TEXTS * sum(w * (WORDS - w + 1) for w in WIDTHS)
+
+
+def tile_textheading_pa_s_kernel(tc, words_emb, W2, b2, W3, b3, W4, b4, out):
+    nc = tc.nc
+    weights = {2: W2, 3: W3, 4: W4}
+    biases = {2: b2, 3: b3, 4: b4}
+
+    first_slab = {}
+    n_slabs = 0
+    for width in WIDTHS:
+        first_slab[width] = n_slabs
+        n_slabs += PARITIES * width
+
+    with ExitStack() as ctx:
+        keep = ctx.enter_context(tc.tile_pool(name="keep", bufs=1))
+        flip = ctx.enter_context(tc.psum_pool(name="flip", bufs=4))
+        sums = ctx.enter_context(tc.psum_pool(name="sums", bufs=1))
+
+        x_rows = keep.tile([P, FEATURES], BF16)
+        nc.sync.dma_start(out=x_rows[:], in_=words_emb.rearrange("n t d -> (n t) d"))
+        w_rows = keep.tile([P, n_slabs, FEATURES], BF16)
+        for width in WIDTHS:
+            by_parity = weights[width].rearrange("(q j) k d -> q j k d", j=PARITIES)
+            for j in range(PARITIES):
+                start = first_slab[width] + j * width
+                nc.sync.dma_start(out=w_rows[:, start : start + width, :], in_=by_parity[:, j, :, :])
+        b_rows = keep.tile([P, FILTERS], BF16)
+        nc.vector.memset(b_rows[:], 0.0)
+        for i, width in enumerate(WIDTHS):
+            nc.scalar.dma_start(out=b_rows[i : i + 1, :], in_=biases[width].rearrange("(o f) -> o f", o=1))
+
+        identity = keep.tile([P, P], F32)
+        make_identity(nc, identity[:])
+        ones = keep.tile([P, P], F32)
+        nc.vector.memset(ones[:], 1.0)
+        table_warmer = keep.tile([P, 1], F32)
+        nc.scalar.activation(out=table_warmer[:], in_=ones[:, 0:1], func=ACT.Abs_reciprocal_sqrt)
+
+        x_grouped = keep.tile([P, SHIFTS * TOKENS * PACK], BF16, align_bytes=64)
+        x_codes = keep.tile([P, SHIFTS * TOKENS], U32, align_bytes=64)
+        x_scales = keep.tile([P, SHIFTS * TOKENS], U8, align_bytes=64)
+        x_pairs = x_grouped[:].bitcast(F32).rearrange("p (s t u) -> p s t u", s=SHIFTS, u=HALVES)
+        nc.vector.memset(x_pairs[:, 1:, TOKENS - SHIFTS + 1 :, :], 0.0)
+        x_flipped = flip.tile([P, SLABS_PER_BANK * HALVES, P], F32, name="x_flipped", tag="flipped")
+        for u in range(HALVES):
+            nc.tensor.transpose(x_flipped[:, u, :], x_rows[:].bitcast(F32)[:, u * P : (u + 1) * P], identity[:])
+        nc.vector.tensor_copy(out=x_pairs[:, 0, :, :], in_=x_flipped[:, 0:HALVES, :].rearrange("p u t -> p t u"))
+        for s in range(1, SHIFTS):
+            nc.vector.tensor_copy(out=x_pairs[:, s, : TOKENS - s, :], in_=x_pairs[:, 0, s:, :])
+        nc.vector.quantize_mx(out=x_codes[:].bitcast(FP8X4), scales=x_scales[:], in_=x_grouped[:])
+
+        b_flipped = flip.tile([P, SLABS_PER_BANK * HALVES, P], F32, name="b_flipped", tag="flipped")
+        nc.tensor.transpose(b_flipped[:, 0, :], b_rows[:].bitcast(F32), identity[:])
+        bias = keep.tile([P, len(WIDTHS) * PARITIES], F32)
+        nc.vector.tensor_copy(out=bias[:], in_=b_flipped[:, 0, 0 : len(WIDTHS)].bitcast(BF16))
+
+        w_pairs_rows = w_rows[:].rearrange("q b d -> q (b d)").bitcast(F32)
+        w_grouped = keep.tile([P, n_slabs * SLAB_COLS], BF16, align_bytes=64)
+        w_codes = keep.tile([P, n_slabs * P], U32, align_bytes=64)
+        w_scales = keep.tile([P, n_slabs * P], U8, align_bytes=64)
+
+        def transpose_and_quantise(bank):
+            flipped = flip.tile([P, SLABS_PER_BANK * HALVES, P], F32, name="flipped", tag="flipped")
+            for t in range(SLABS_PER_BANK * HALVES):
+                first = (bank * SLABS_PER_BANK * HALVES + t) * P
+                nc.tensor.transpose(flipped[:, t, :], w_pairs_rows[:, first : first + P], identity[:])
+            grouped = w_grouped[:, bank * SLABS_PER_BANK * SLAB_COLS : (bank + 1) * SLABS_PER_BANK * SLAB_COLS]
+            nc.scalar.copy(
+                out=grouped.bitcast(F32).rearrange("p (b q u) -> p b q u", b=SLABS_PER_BANK, u=HALVES),
+                in_=flipped[:].rearrange("p (b u) q -> p b q u", u=HALVES),
+            )
+            cols = slice(bank * SLABS_PER_BANK * P, (bank + 1) * SLABS_PER_BANK * P)
+            nc.vector.quantize_mx(out=w_codes[:, cols].bitcast(FP8X4), scales=w_scales[:, cols], in_=grouped)
+
+        code = keep.tile([P, PARITIES, TOKENS], F32)
+
+        def by_text(ap, positions):
+            return ap.rearrange("q (n p) -> q n p", p=WORDS)[:, :, :positions]
+
+        def convolve_and_merge(width):
+            conv = sums.tile([P, PARITIES, TOKENS], F32, name="conv%d" % width)
+            for j in range(PARITIES):
+                for k in range(width):
+                    slab = slice((first_slab[width] + j * width + k) * P, (first_slab[width] + j * width + k + 1) * P)
+                    shifted = slice(k * TOKENS, (k + 1) * TOKENS)
+                    nc.tensor.matmul_mx(
+                        out=conv[:, j, :],
+                        lhsT=w_codes[:, slab].bitcast(FP8X4),
+                        lhsT_scale=w_scales[:, slab],
+                        rhs=x_codes[:, shifted].bitcast(FP8X4),
+                        rhs_scale=x_scales[:, shifted],
+                        start=(k == 0),
+                        stop=(k == width - 1),
+                    )
+            for j in range(PARITIES):
+                column = WIDTHS.index(width) * PARITIES + j
+                if width == WIDTHS[0]:
+                    nc.scalar.activation(
+                        out=code[:, j, :], in_=conv[:, j, :], func=ACT.Relu, bias=bias[:, column : column + 1]
+                    )
+                else:
+                    positions = WORDS - width + 1
+                    nc.vector.scalar_tensor_tensor(
+                        out=by_text(code[:, j, :], positions),
+                        in0=by_text(conv[:, j, :], positions),
+                        scalar=bias[:, column : column + 1],
+                        in1=by_text(code[:, j, :], positions),
+                        op0=ALU.add,
+                        op1=ALU.max,
+                    )
+
+        previous = None
+        for width in WIDTHS:
+            first_bank = first_slab[width] // SLABS_PER_BANK
+            for bank in range(first_bank, first_bank + PARITIES * width // SLABS_PER_BANK):
+                transpose_and_quantise(bank)
+            if previous is not None:
+                convolve_and_merge(previous)
+            previous = width
+        convolve_and_merge(previous)
+
+        squares = keep.tile([P, PARITIES, TOKENS], F32)
+        square_sum = sums.tile([P, TOKENS], F32)
+        for j in range(PARITIES):
+            nc.vector.tensor_mul(squares[:, j, :], code[:, j, :], code[:, j, :])
+            nc.tensor.matmul(
+                out=square_sum[:], lhsT=ones[:], rhs=squares[:, j, :], start=(j == 0), stop=(j == PARITIES - 1)
+            )
+        inverse_norm = keep.tile([P, TOKENS], F32)
+        nc.scalar.activation(out=inverse_norm[:], in_=square_sum[:], func=ACT.Abs_reciprocal_sqrt)
+        result = keep.tile([P, TEXTS, PARITIES, POSITIONS], F32)
+        for j in range(PARITIES):
+            nc.vector.scalar_tensor_tensor(
+                out=result[:, :, j, :],
+                in0=by_text(inverse_norm[:], POSITIONS),
+                scalar=1.0 / EPS,
+                in1=by_text(code[:, j, :], POSITIONS),
+                op0=ALU.min,
+                op1=ALU.mult,
+            )
+        nc.sync.dma_start(
+            out=out.rearrange("n (q j) p -> q n (j p)", j=PARITIES),
+            in_=result[:].rearrange("q n j p -> q n (j p)"),
+        )

@@ -15,15 +15,16 @@ P = 128
 PACK = 4
 TEXTS, WORDS, FEATURES, FILTERS = 4, 32, 512, 256
 TOKENS = TEXTS * WORDS
-WIDTHS = (2, 3, 4)
+WIDTHS = (4, 2, 3)
 SHIFTS = max(WIDTHS)
 PARITIES = FILTERS // P
 POSITIONS = WORDS - min(WIDTHS) + 1
 EPS = 1e-12
-PAIRS = FEATURES // 2
-HALVES = PAIRS // P
+HALVES = FEATURES // 2 // P
 SLABS_PER_BANK = 2
-SLAB_COLS = P * PACK
+BANK_COLS = SLABS_PER_BANK * FEATURES
+BANKS_PER_STEP = 2
+WARM_PASSES = 16
 
 assert TOKENS == P and FEATURES == P * PACK
 
@@ -35,29 +36,54 @@ def tile_textheading_pa_s_kernel(tc, words_emb, W2, b2, W3, b3, W4, b4, out):
     weights = {2: W2, 3: W3, 4: W4}
     biases = {2: b2, 3: b3, 4: b4}
 
-    first_slab = {}
-    n_slabs = 0
-    for width in WIDTHS:
-        first_slab[width] = n_slabs
-        n_slabs += PARITIES * width
+    slabs = [(width, j, k) for width in WIDTHS for j in range(PARITIES) for k in range(width)]
+    n_banks = len(slabs) // SLABS_PER_BANK
+
+    def banks_of(step):
+        return [b for b in range(step * BANKS_PER_STEP, (step + 1) * BANKS_PER_STEP) if 0 <= b < n_banks]
 
     with ExitStack() as ctx:
         keep = ctx.enter_context(tc.tile_pool(name="keep", bufs=1))
-        flip = ctx.enter_context(tc.psum_pool(name="flip", bufs=4))
+        flip = ctx.enter_context(tc.psum_pool(name="flip", bufs=2 * BANKS_PER_STEP))
         sums = ctx.enter_context(tc.psum_pool(name="sums", bufs=1))
+        ctx.enter_context(tc.manual_schedule())
 
-        x_rows = keep.tile([P, FEATURES], BF16)
-        nc.sync.dma_start(out=x_rows[:], in_=words_emb.rearrange("n t d -> (n t) d"))
-        w_rows = keep.tile([P, n_slabs, FEATURES], BF16)
-        for width in WIDTHS:
-            by_parity = weights[width].rearrange("(q j) k d -> q j k d", j=PARITIES)
-            for j in range(PARITIES):
-                start = first_slab[width] + j * width
-                nc.sync.dma_start(out=w_rows[:, start : start + width, :], in_=by_parity[:, j, :, :])
         b_rows = keep.tile([P, FILTERS], BF16)
-        nc.vector.memset(b_rows[:], 0.0)
+        nc.gpsimd.memset(b_rows[:], 0.0)
         for i, width in enumerate(WIDTHS):
             nc.scalar.dma_start(out=b_rows[i : i + 1, :], in_=biases[width].rearrange("(o f) -> o f", o=1))
+        x_rows = keep.tile([P, FEATURES], BF16)
+        nc.sync.dma_start(out=x_rows[:], in_=words_emb.rearrange("n t d -> (n t) d"))
+        w_rows = []
+        for width in WIDTHS:
+            runs = weights[width].rearrange("(q j) k d -> q (j k d)", j=PARITIES)
+            width_banks = PARITIES * width // SLABS_PER_BANK
+            for first in range(0, width_banks, BANKS_PER_STEP):
+                last = min(first + BANKS_PER_STEP, width_banks)
+                rows = keep.tile([P, (last - first) * BANK_COLS], BF16, name="w_rows%d" % len(w_rows))
+                nc.sync.dma_start(out=rows[:], in_=runs[:, first * BANK_COLS : last * BANK_COLS])
+                w_rows.append(rows)
+
+        zeros = keep.tile([P, P * PACK], BF16, align_bytes=64)
+        zero_codes = keep.tile([P, P], U32, align_bytes=64)
+        zero_scales = keep.tile([P, P], U8, align_bytes=64)
+        nc.vector.memset(zeros[:], 0.0)
+        nc.vector.quantize_mx(out=zero_codes[:].bitcast(FP8X4), scales=zero_scales[:], in_=zeros[:])
+        idle_sums = sums.tile([P, P], F32, name="idle_sums", tag="norm")
+
+        def idle(passes):
+            for i in range(passes):
+                nc.tensor.matmul_mx(
+                    out=idle_sums[:],
+                    lhsT=zero_codes[:].bitcast(FP8X4),
+                    lhsT_scale=zero_scales[:],
+                    rhs=zero_codes[:].bitcast(FP8X4),
+                    rhs_scale=zero_scales[:],
+                    start=True,
+                    stop=True,
+                )
+
+        idle(WARM_PASSES)
 
         identity = keep.tile([P, P], F32)
         make_identity(nc, identity[:])
@@ -65,6 +91,8 @@ def tile_textheading_pa_s_kernel(tc, words_emb, W2, b2, W3, b3, W4, b4, out):
         nc.vector.memset(ones[:], 1.0)
         table_warmer = keep.tile([P, 1], F32)
         nc.scalar.activation(out=table_warmer[:], in_=ones[:, 0:1], func=ACT.Abs_reciprocal_sqrt)
+        code = keep.tile([P, PARITIES, TOKENS], F32)
+        nc.vector.memset(code[:], 0.0)
 
         x_grouped = keep.tile([P, SHIFTS * TOKENS * PACK], BF16, align_bytes=64)
         x_codes = keep.tile([P, SHIFTS * TOKENS], U32, align_bytes=64)
@@ -74,90 +102,97 @@ def tile_textheading_pa_s_kernel(tc, words_emb, W2, b2, W3, b3, W4, b4, out):
         x_flipped = flip.tile([P, SLABS_PER_BANK * HALVES, P], F32, name="x_flipped", tag="flipped")
         for u in range(HALVES):
             nc.tensor.transpose(x_flipped[:, u, :], x_rows[:].bitcast(F32)[:, u * P : (u + 1) * P], identity[:])
+        b_flipped = flip.tile([P, SLABS_PER_BANK * HALVES, P], F32, name="b_flipped", tag="flipped")
+        nc.tensor.transpose(b_flipped[:, 0, :], b_rows[:].bitcast(F32), identity[:])
         nc.vector.tensor_copy(out=x_pairs[:, 0, :, :], in_=x_flipped[:, 0:HALVES, :].rearrange("p u t -> p t u"))
+        bias = keep.tile([P, len(WIDTHS) * PARITIES], F32)
+        nc.vector.tensor_copy(out=bias[:], in_=b_flipped[:, 0, 0 : len(WIDTHS)].bitcast(BF16))
         for s in range(1, SHIFTS):
             nc.vector.tensor_copy(out=x_pairs[:, s, : TOKENS - s, :], in_=x_pairs[:, 0, s:, :])
         nc.vector.quantize_mx(out=x_codes[:].bitcast(FP8X4), scales=x_scales[:], in_=x_grouped[:])
 
-        b_flipped = flip.tile([P, SLABS_PER_BANK * HALVES, P], F32, name="b_flipped", tag="flipped")
-        nc.tensor.transpose(b_flipped[:, 0, :], b_rows[:].bitcast(F32), identity[:])
-        bias = keep.tile([P, len(WIDTHS) * PARITIES], F32)
-        nc.vector.tensor_copy(out=bias[:], in_=b_flipped[:, 0, 0 : len(WIDTHS)].bitcast(BF16))
+        w_grouped = []
+        w_codes = []
+        w_scales = []
+        for bank in range(n_banks):
+            w_grouped.append(keep.tile([P, BANK_COLS], BF16, name="w_grouped%d" % bank, align_bytes=64))
+            w_codes.append(keep.tile([P, SLABS_PER_BANK * P], U32, name="w_codes%d" % bank, align_bytes=64))
+            w_scales.append(keep.tile([P, SLABS_PER_BANK * P], U8, name="w_scales%d" % bank, align_bytes=64))
+        conv = {}
+        for width in WIDTHS:
+            conv[width] = sums.tile([P, PARITIES, TOKENS], F32, name="conv%d" % width)
 
-        w_pairs_rows = w_rows[:].rearrange("q b d -> q (b d)").bitcast(F32)
-        w_grouped = keep.tile([P, n_slabs * SLAB_COLS], BF16, align_bytes=64)
-        w_codes = keep.tile([P, n_slabs * P], U32, align_bytes=64)
-        w_scales = keep.tile([P, n_slabs * P], U8, align_bytes=64)
-
-        def transpose_and_quantise(bank):
+        def transpose(bank):
+            step, place = divmod(bank, BANKS_PER_STEP)
+            words = w_rows[step][:, place * BANK_COLS : (place + 1) * BANK_COLS].bitcast(F32)
             flipped = flip.tile([P, SLABS_PER_BANK * HALVES, P], F32, name="flipped", tag="flipped")
             for t in range(SLABS_PER_BANK * HALVES):
-                first = (bank * SLABS_PER_BANK * HALVES + t) * P
-                nc.tensor.transpose(flipped[:, t, :], w_pairs_rows[:, first : first + P], identity[:])
-            grouped = w_grouped[:, bank * SLABS_PER_BANK * SLAB_COLS : (bank + 1) * SLABS_PER_BANK * SLAB_COLS]
+                nc.tensor.transpose(flipped[:, t, :], words[:, t * P : (t + 1) * P], identity[:])
             nc.scalar.copy(
-                out=grouped.bitcast(F32).rearrange("p (b q u) -> p b q u", b=SLABS_PER_BANK, u=HALVES),
+                out=w_grouped[bank][:].bitcast(F32).rearrange("p (b q u) -> p b q u", b=SLABS_PER_BANK, u=HALVES),
                 in_=flipped[:].rearrange("p (b u) q -> p b q u", u=HALVES),
             )
-            cols = slice(bank * SLABS_PER_BANK * P, (bank + 1) * SLABS_PER_BANK * P)
-            nc.vector.quantize_mx(out=w_codes[:, cols].bitcast(FP8X4), scales=w_scales[:, cols], in_=grouped)
 
-        code = keep.tile([P, PARITIES, TOKENS], F32)
+        def quantise(bank):
+            nc.vector.quantize_mx(out=w_codes[bank][:].bitcast(FP8X4), scales=w_scales[bank][:], in_=w_grouped[bank][:])
+
+        def multiply(bank):
+            for place in range(SLABS_PER_BANK):
+                width, j, k = slabs[bank * SLABS_PER_BANK + place]
+                slab = slice(place * P, (place + 1) * P)
+                shifted = slice(k * TOKENS, (k + 1) * TOKENS)
+                nc.tensor.matmul_mx(
+                    out=conv[width][:, j, :],
+                    lhsT=w_codes[bank][:, slab].bitcast(FP8X4),
+                    lhsT_scale=w_scales[bank][:, slab],
+                    rhs=x_codes[:, shifted].bitcast(FP8X4),
+                    rhs_scale=x_scales[:, shifted],
+                    start=(k == 0),
+                    stop=(k == width - 1),
+                )
 
         def by_text(ap, positions):
             return ap.rearrange("q (n p) -> q n p", p=WORDS)[:, :, :positions]
 
-        def convolve_and_merge(width):
-            conv = sums.tile([P, PARITIES, TOKENS], F32, name="conv%d" % width)
-            for j in range(PARITIES):
-                for k in range(width):
-                    slab = slice((first_slab[width] + j * width + k) * P, (first_slab[width] + j * width + k + 1) * P)
-                    shifted = slice(k * TOKENS, (k + 1) * TOKENS)
-                    nc.tensor.matmul_mx(
-                        out=conv[:, j, :],
-                        lhsT=w_codes[:, slab].bitcast(FP8X4),
-                        lhsT_scale=w_scales[:, slab],
-                        rhs=x_codes[:, shifted].bitcast(FP8X4),
-                        rhs_scale=x_scales[:, shifted],
-                        start=(k == 0),
-                        stop=(k == width - 1),
-                    )
-            for j in range(PARITIES):
-                column = WIDTHS.index(width) * PARITIES + j
-                if width == WIDTHS[0]:
-                    nc.scalar.activation(
-                        out=code[:, j, :], in_=conv[:, j, :], func=ACT.Relu, bias=bias[:, column : column + 1]
-                    )
-                else:
+        def merge(bank):
+            for place in range(SLABS_PER_BANK):
+                width, j, k = slabs[bank * SLABS_PER_BANK + place]
+                if k == width - 1:
                     positions = WORDS - width + 1
+                    column = WIDTHS.index(width) * PARITIES + j
                     nc.vector.scalar_tensor_tensor(
                         out=by_text(code[:, j, :], positions),
-                        in0=by_text(conv[:, j, :], positions),
+                        in0=by_text(conv[width][:, j, :], positions),
                         scalar=bias[:, column : column + 1],
                         in1=by_text(code[:, j, :], positions),
                         op0=ALU.add,
                         op1=ALU.max,
                     )
 
-        previous = None
-        for width in WIDTHS:
-            first_bank = first_slab[width] // SLABS_PER_BANK
-            for bank in range(first_bank, first_bank + PARITIES * width // SLABS_PER_BANK):
-                transpose_and_quantise(bank)
-            if previous is not None:
-                convolve_and_merge(previous)
-            previous = width
-        convolve_and_merge(previous)
+        n_steps = len(w_rows)
+        for step in range(n_steps + 2):
+            for bank in banks_of(step):
+                transpose(bank)
+            for bank in banks_of(step - 1):
+                quantise(bank)
+            if step == 0:
+                idle(BANKS_PER_STEP * SLABS_PER_BANK)
+            for bank in banks_of(step - 1):
+                multiply(bank)
+            for bank in banks_of(step - 2):
+                merge(bank)
 
         squares = keep.tile([P, PARITIES, TOKENS], F32)
-        square_sum = sums.tile([P, TOKENS], F32)
+        square_sum = sums.tile([P, TOKENS], F32, name="square_sum", tag="norm")
         for j in range(PARITIES):
-            nc.vector.tensor_mul(squares[:, j, :], code[:, j, :], code[:, j, :])
+            nc.scalar.activation(out=squares[:, j, :], in_=code[:, j, :], func=ACT.Square)
             nc.tensor.matmul(
                 out=square_sum[:], lhsT=ones[:], rhs=squares[:, j, :], start=(j == 0), stop=(j == PARITIES - 1)
             )
         inverse_norm = keep.tile([P, TOKENS], F32)
-        nc.scalar.activation(out=inverse_norm[:], in_=square_sum[:], func=ACT.Abs_reciprocal_sqrt)
+        nc.scalar.activation(
+            out=by_text(inverse_norm[:], POSITIONS), in_=by_text(square_sum[:], POSITIONS), func=ACT.Abs_reciprocal_sqrt
+        )
         result = keep.tile([P, TEXTS, PARITIES, POSITIONS], F32)
         for j in range(PARITIES):
             nc.vector.scalar_tensor_tensor(

@@ -15,16 +15,19 @@ P = 128
 PACK = 4
 TEXTS, WORDS, FEATURES, FILTERS = 4, 32, 512, 256
 TOKENS = TEXTS * WORDS
-WIDTHS = (4, 2, 3)
+WIDTHS = (4, 3, 2)
 SHIFTS = max(WIDTHS)
 PARITIES = FILTERS // P
 POSITIONS = WORDS - min(WIDTHS) + 1
 EPS = 1e-12
-HALVES = FEATURES // 2 // P
+PAIRS = FEATURES // 2
+HALVES = PAIRS // P
 SLABS_PER_BANK = 2
-BANK_COLS = SLABS_PER_BANK * FEATURES
-BANKS_PER_STEP = 2
-WARM_PASSES = 16
+SLAB_COLS = P * PACK
+VECTOR_EMPTIES_EVERY = 4
+WARM_PASSES = 4
+WARM_COLS = 512
+CONV_LAG = 2
 
 assert TOKENS == P and FEATURES == P * PACK
 
@@ -36,20 +39,20 @@ def tile_textheading_pa_s_kernel(tc, words_emb, W2, b2, W3, b3, W4, b4, out):
     weights = {2: W2, 3: W3, 4: W4}
     biases = {2: b2, 3: b3, 4: b4}
 
-    slabs = [(width, j, k) for width in WIDTHS for j in range(PARITIES) for k in range(width)]
-    n_banks = len(slabs) // SLABS_PER_BANK
-
-    def banks_of(step):
-        return [b for b in range(step * BANKS_PER_STEP, (step + 1) * BANKS_PER_STEP) if 0 <= b < n_banks]
+    first_slab = {}
+    n_slabs = 0
+    for width in WIDTHS:
+        first_slab[width] = n_slabs
+        n_slabs += PARITIES * width
 
     with ExitStack() as ctx:
         keep = ctx.enter_context(tc.tile_pool(name="keep", bufs=1))
-        flip = ctx.enter_context(tc.psum_pool(name="flip", bufs=2 * BANKS_PER_STEP))
+        flip = ctx.enter_context(tc.psum_pool(name="flip", bufs=4))
         sums = ctx.enter_context(tc.psum_pool(name="sums", bufs=1))
         ctx.enter_context(tc.manual_schedule())
 
         b_rows = keep.tile([P, FILTERS], BF16)
-        nc.gpsimd.memset(b_rows[:], 0.0)
+        nc.vector.memset(b_rows[:], 0.0)
         for i, width in enumerate(WIDTHS):
             nc.scalar.dma_start(out=b_rows[i : i + 1, :], in_=biases[width].rearrange("(o f) -> o f", o=1))
         x_rows = keep.tile([P, FEATURES], BF16)
@@ -57,33 +60,10 @@ def tile_textheading_pa_s_kernel(tc, words_emb, W2, b2, W3, b3, W4, b4, out):
         w_rows = []
         for width in WIDTHS:
             runs = weights[width].rearrange("(q j) k d -> q (j k d)", j=PARITIES)
-            width_banks = PARITIES * width // SLABS_PER_BANK
-            for first in range(0, width_banks, BANKS_PER_STEP):
-                last = min(first + BANKS_PER_STEP, width_banks)
-                rows = keep.tile([P, (last - first) * BANK_COLS], BF16, name="w_rows%d" % len(w_rows))
-                nc.sync.dma_start(out=rows[:], in_=runs[:, first * BANK_COLS : last * BANK_COLS])
+            for first in range(0, PARITIES * width * FEATURES, SLABS_PER_BANK * FEATURES):
+                rows = keep.tile([P, SLABS_PER_BANK * FEATURES], BF16, name="w_rows%d" % len(w_rows))
+                nc.sync.dma_start(out=rows[:], in_=runs[:, first : first + SLABS_PER_BANK * FEATURES])
                 w_rows.append(rows)
-
-        zeros = keep.tile([P, P * PACK], BF16, align_bytes=64)
-        zero_codes = keep.tile([P, P], U32, align_bytes=64)
-        zero_scales = keep.tile([P, P], U8, align_bytes=64)
-        nc.vector.memset(zeros[:], 0.0)
-        nc.vector.quantize_mx(out=zero_codes[:].bitcast(FP8X4), scales=zero_scales[:], in_=zeros[:])
-        idle_sums = sums.tile([P, P], F32, name="idle_sums", tag="norm")
-
-        def idle(passes):
-            for i in range(passes):
-                nc.tensor.matmul_mx(
-                    out=idle_sums[:],
-                    lhsT=zero_codes[:].bitcast(FP8X4),
-                    lhsT_scale=zero_scales[:],
-                    rhs=zero_codes[:].bitcast(FP8X4),
-                    rhs_scale=zero_scales[:],
-                    start=True,
-                    stop=True,
-                )
-
-        idle(WARM_PASSES)
 
         identity = keep.tile([P, P], F32)
         make_identity(nc, identity[:])
@@ -91,8 +71,23 @@ def tile_textheading_pa_s_kernel(tc, words_emb, W2, b2, W3, b3, W4, b4, out):
         nc.vector.memset(ones[:], 1.0)
         table_warmer = keep.tile([P, 1], F32)
         nc.scalar.activation(out=table_warmer[:], in_=ones[:, 0:1], func=ACT.Abs_reciprocal_sqrt)
-        code = keep.tile([P, PARITIES, TOKENS], F32)
-        nc.vector.memset(code[:], 0.0)
+
+        zeros = keep.tile([P, WARM_COLS * PACK], BF16, align_bytes=64)
+        zero_codes = keep.tile([P, WARM_COLS], U32, align_bytes=64)
+        zero_scales = keep.tile([P, WARM_COLS], U8, align_bytes=64)
+        nc.vector.memset(zeros[:].bitcast(F32), 0.0)
+        nc.vector.quantize_mx(out=zero_codes[:].bitcast(FP8X4), scales=zero_scales[:], in_=zeros[:])
+        idle_sums = flip.tile([P, WARM_COLS], F32, name="idle_sums", tag="flipped")
+        for i in range(WARM_PASSES):
+            nc.tensor.matmul_mx(
+                out=idle_sums[:],
+                lhsT=zero_codes[:, :P].bitcast(FP8X4),
+                lhsT_scale=zero_scales[:, :P],
+                rhs=zero_codes[:].bitcast(FP8X4),
+                rhs_scale=zero_scales[:],
+                start=True,
+                stop=True,
+            )
 
         x_grouped = keep.tile([P, SHIFTS * TOKENS * PACK], BF16, align_bytes=64)
         x_codes = keep.tile([P, SHIFTS * TOKENS], U32, align_bytes=64)
@@ -102,88 +97,93 @@ def tile_textheading_pa_s_kernel(tc, words_emb, W2, b2, W3, b3, W4, b4, out):
         x_flipped = flip.tile([P, SLABS_PER_BANK * HALVES, P], F32, name="x_flipped", tag="flipped")
         for u in range(HALVES):
             nc.tensor.transpose(x_flipped[:, u, :], x_rows[:].bitcast(F32)[:, u * P : (u + 1) * P], identity[:])
-        b_flipped = flip.tile([P, SLABS_PER_BANK * HALVES, P], F32, name="b_flipped", tag="flipped")
-        nc.tensor.transpose(b_flipped[:, 0, :], b_rows[:].bitcast(F32), identity[:])
         nc.vector.tensor_copy(out=x_pairs[:, 0, :, :], in_=x_flipped[:, 0:HALVES, :].rearrange("p u t -> p t u"))
-        bias = keep.tile([P, len(WIDTHS) * PARITIES], F32)
-        nc.vector.tensor_copy(out=bias[:], in_=b_flipped[:, 0, 0 : len(WIDTHS)].bitcast(BF16))
         for s in range(1, SHIFTS):
             nc.vector.tensor_copy(out=x_pairs[:, s, : TOKENS - s, :], in_=x_pairs[:, 0, s:, :])
         nc.vector.quantize_mx(out=x_codes[:].bitcast(FP8X4), scales=x_scales[:], in_=x_grouped[:])
 
+        b_flipped = flip.tile([P, SLABS_PER_BANK * HALVES, P], F32, name="b_flipped", tag="flipped")
+        nc.tensor.transpose(b_flipped[:, 0, :], b_rows[:].bitcast(F32), identity[:])
+        bias = keep.tile([P, len(WIDTHS) * PARITIES], F32)
+        nc.vector.tensor_copy(out=bias[:], in_=b_flipped[:, 0, 0 : len(WIDTHS)].bitcast(BF16))
+
+        n_banks = n_slabs // SLABS_PER_BANK
         w_grouped = []
         w_codes = []
         w_scales = []
         for bank in range(n_banks):
-            w_grouped.append(keep.tile([P, BANK_COLS], BF16, name="w_grouped%d" % bank, align_bytes=64))
+            w_grouped.append(keep.tile([P, SLABS_PER_BANK * SLAB_COLS], BF16, name="w_grouped%d" % bank, align_bytes=64))
             w_codes.append(keep.tile([P, SLABS_PER_BANK * P], U32, name="w_codes%d" % bank, align_bytes=64))
             w_scales.append(keep.tile([P, SLABS_PER_BANK * P], U8, name="w_scales%d" % bank, align_bytes=64))
-        conv = {}
-        for width in WIDTHS:
-            conv[width] = sums.tile([P, PARITIES, TOKENS], F32, name="conv%d" % width)
 
         def transpose(bank):
-            step, place = divmod(bank, BANKS_PER_STEP)
-            words = w_rows[step][:, place * BANK_COLS : (place + 1) * BANK_COLS].bitcast(F32)
             flipped = flip.tile([P, SLABS_PER_BANK * HALVES, P], F32, name="flipped", tag="flipped")
             for t in range(SLABS_PER_BANK * HALVES):
-                nc.tensor.transpose(flipped[:, t, :], words[:, t * P : (t + 1) * P], identity[:])
-            nc.scalar.copy(
-                out=w_grouped[bank][:].bitcast(F32).rearrange("p (b q u) -> p b q u", b=SLABS_PER_BANK, u=HALVES),
-                in_=flipped[:].rearrange("p (b u) q -> p b q u", u=HALVES),
-            )
+                nc.tensor.transpose(flipped[:, t, :], w_rows[bank][:].bitcast(F32)[:, t * P : (t + 1) * P], identity[:])
+            pairs = w_grouped[bank][:].bitcast(F32).rearrange("p (b q u) -> p b q u", b=SLABS_PER_BANK, u=HALVES)
+            source = flipped[:].rearrange("p (b u) q -> p b q u", u=HALVES)
+            if bank % VECTOR_EMPTIES_EVERY == VECTOR_EMPTIES_EVERY - 1:
+                nc.vector.tensor_copy(out=pairs, in_=source)
+            else:
+                nc.scalar.copy(out=pairs, in_=source)
 
         def quantise(bank):
             nc.vector.quantize_mx(out=w_codes[bank][:].bitcast(FP8X4), scales=w_scales[bank][:], in_=w_grouped[bank][:])
 
-        def multiply(bank):
-            for place in range(SLABS_PER_BANK):
-                width, j, k = slabs[bank * SLABS_PER_BANK + place]
-                slab = slice(place * P, (place + 1) * P)
-                shifted = slice(k * TOKENS, (k + 1) * TOKENS)
-                nc.tensor.matmul_mx(
-                    out=conv[width][:, j, :],
-                    lhsT=w_codes[bank][:, slab].bitcast(FP8X4),
-                    lhsT_scale=w_scales[bank][:, slab],
-                    rhs=x_codes[:, shifted].bitcast(FP8X4),
-                    rhs_scale=x_scales[:, shifted],
-                    start=(k == 0),
-                    stop=(k == width - 1),
-                )
+        code = keep.tile([P, PARITIES, TOKENS], F32)
+        nc.vector.memset(code[:], 0.0)
 
         def by_text(ap, positions):
             return ap.rearrange("q (n p) -> q n p", p=WORDS)[:, :, :positions]
 
-        def merge(bank):
-            for place in range(SLABS_PER_BANK):
-                width, j, k = slabs[bank * SLABS_PER_BANK + place]
-                if k == width - 1:
-                    positions = WORDS - width + 1
-                    column = WIDTHS.index(width) * PARITIES + j
-                    nc.vector.scalar_tensor_tensor(
-                        out=by_text(code[:, j, :], positions),
-                        in0=by_text(conv[width][:, j, :], positions),
-                        scalar=bias[:, column : column + 1],
-                        in1=by_text(code[:, j, :], positions),
-                        op0=ALU.add,
-                        op1=ALU.max,
+        conv = {}
+        for width in WIDTHS:
+            conv[width] = sums.tile([P, PARITIES, TOKENS], F32, name="conv%d" % width)
+
+        def convolve(width):
+            for j in range(PARITIES):
+                for k in range(width):
+                    bank, place = divmod(first_slab[width] + j * width + k, SLABS_PER_BANK)
+                    slab = slice(place * P, (place + 1) * P)
+                    shifted = slice(k * TOKENS, (k + 1) * TOKENS)
+                    nc.tensor.matmul_mx(
+                        out=conv[width][:, j, :],
+                        lhsT=w_codes[bank][:, slab].bitcast(FP8X4),
+                        lhsT_scale=w_scales[bank][:, slab],
+                        rhs=x_codes[:, shifted].bitcast(FP8X4),
+                        rhs_scale=x_scales[:, shifted],
+                        start=(k == 0),
+                        stop=(k == width - 1),
                     )
 
-        n_steps = len(w_rows)
-        for step in range(n_steps + 2):
-            for bank in banks_of(step):
-                transpose(bank)
-            for bank in banks_of(step - 1):
-                quantise(bank)
-            if step == 0:
-                idle(BANKS_PER_STEP * SLABS_PER_BANK)
-            for bank in banks_of(step - 1):
-                multiply(bank)
-            for bank in banks_of(step - 2):
-                merge(bank)
+        def merge(width):
+            positions = WORDS - width + 1
+            for j in range(PARITIES):
+                column = WIDTHS.index(width) * PARITIES + j
+                nc.vector.scalar_tensor_tensor(
+                    out=by_text(code[:, j, :], positions),
+                    in0=by_text(conv[width][:, j, :], positions),
+                    scalar=bias[:, column : column + 1],
+                    in1=by_text(code[:, j, :], positions),
+                    op0=ALU.add,
+                    op1=ALU.max,
+                )
+
+        last_bank = {}
+        for width in WIDTHS:
+            last_bank[(first_slab[width] + PARITIES * width) // SLABS_PER_BANK - 1] = width
+        for step in range(n_banks + CONV_LAG + 1):
+            if step < n_banks:
+                transpose(step)
+            if 0 <= step - 1 < n_banks:
+                quantise(step - 1)
+            if step - CONV_LAG in last_bank:
+                convolve(last_bank[step - CONV_LAG])
+            if step - CONV_LAG - 1 in last_bank:
+                merge(last_bank[step - CONV_LAG - 1])
 
         squares = keep.tile([P, PARITIES, TOKENS], F32)
-        square_sum = sums.tile([P, TOKENS], F32, name="square_sum", tag="norm")
+        square_sum = sums.tile([P, TOKENS], F32)
         for j in range(PARITIES):
             nc.scalar.activation(out=squares[:, j, :], in_=code[:, j, :], func=ACT.Square)
             nc.tensor.matmul(

from contextlib import ExitStack

import concourse.mybir as mybir
from concourse.masks import make_identity

F32 = mybir.dt.float32
BF16 = mybir.dt.bfloat16
U32 = mybir.dt.uint32
U8 = mybir.dt.uint8
FP8X4 = mybir.dt.float8_e4m3fn_x4
ALU = mybir.AluOpType
ACT = mybir.ActivationFunctionType

P = 128
PACK = 4
TEXTS, WORDS, FEATURES, FILTERS = 4, 32, 512, 256
TOKENS = TEXTS * WORDS
WIDTHS = (4, 3, 2)
SHIFTS = max(WIDTHS)
PARITIES = FILTERS // P
POSITIONS = WORDS - min(WIDTHS) + 1
EPS = 1e-12
PAIRS = FEATURES // 2
HALVES = PAIRS // P
SLABS_PER_BANK = 2
SLAB_COLS = P * PACK
VECTOR_EMPTIES_EVERY = 4
WARM_PASSES = 4
WARM_COLS = 512
CONV_LAG = 2

assert TOKENS == P and FEATURES == P * PACK

FLOPS = 2 * FEATURES * FILTERS * TEXTS * sum(w * (WORDS - w + 1) for w in WIDTHS)


def tile_textheading_pa_s_kernel(tc, words_emb, W2, b2, W3, b3, W4, b4, out):
    nc = tc.nc
    weights = {2: W2, 3: W3, 4: W4}
    biases = {2: b2, 3: b3, 4: b4}

    first_slab = {}
    n_slabs = 0
    for width in WIDTHS:
        first_slab[width] = n_slabs
        n_slabs += PARITIES * width

    with ExitStack() as ctx:
        keep = ctx.enter_context(tc.tile_pool(name="keep", bufs=1))
        flip = ctx.enter_context(tc.psum_pool(name="flip", bufs=4))
        sums = ctx.enter_context(tc.psum_pool(name="sums", bufs=1))
        ctx.enter_context(tc.manual_schedule())

        b_rows = keep.tile([P, FILTERS], BF16)
        nc.vector.memset(b_rows[:], 0.0)
        for i, width in enumerate(WIDTHS):
            nc.scalar.dma_start(out=b_rows[i : i + 1, :], in_=biases[width].rearrange("(o f) -> o f", o=1))
        x_rows = keep.tile([P, FEATURES], BF16)
        nc.sync.dma_start(out=x_rows[:], in_=words_emb.rearrange("n t d -> (n t) d"))
        w_rows = []
        for width in WIDTHS:
            runs = weights[width].rearrange("(q j) k d -> q (j k d)", j=PARITIES)
            for first in range(0, PARITIES * width * FEATURES, SLABS_PER_BANK * FEATURES):
                rows = keep.tile([P, SLABS_PER_BANK * FEATURES], BF16, name="w_rows%d" % len(w_rows))
                nc.sync.dma_start(out=rows[:], in_=runs[:, first : first + SLABS_PER_BANK * FEATURES])
                w_rows.append(rows)

        identity = keep.tile([P, P], F32)
        make_identity(nc, identity[:])
        ones = keep.tile([P, P], F32)
        nc.vector.memset(ones[:], 1.0)
        table_warmer = keep.tile([P, 1], F32)
        nc.scalar.activation(out=table_warmer[:], in_=ones[:, 0:1], func=ACT.Abs_reciprocal_sqrt)

        zeros = keep.tile([P, WARM_COLS * PACK], BF16, align_bytes=64)
        zero_codes = keep.tile([P, WARM_COLS], U32, align_bytes=64)
        zero_scales = keep.tile([P, WARM_COLS], U8, align_bytes=64)
        nc.vector.memset(zeros[:].bitcast(F32), 0.0)
        nc.vector.quantize_mx(out=zero_codes[:].bitcast(FP8X4), scales=zero_scales[:], in_=zeros[:])
        idle_sums = flip.tile([P, WARM_COLS], F32, name="idle_sums", tag="flipped")
        for i in range(WARM_PASSES):
            nc.tensor.matmul_mx(
                out=idle_sums[:],
                lhsT=zero_codes[:, :P].bitcast(FP8X4),
                lhsT_scale=zero_scales[:, :P],
                rhs=zero_codes[:].bitcast(FP8X4),
                rhs_scale=zero_scales[:],
                start=True,
                stop=True,
            )

        x_grouped = keep.tile([P, SHIFTS * TOKENS * PACK], BF16, align_bytes=64)
        x_codes = keep.tile([P, SHIFTS * TOKENS], U32, align_bytes=64)
        x_scales = keep.tile([P, SHIFTS * TOKENS], U8, align_bytes=64)
        x_pairs = x_grouped[:].bitcast(F32).rearrange("p (s t u) -> p s t u", s=SHIFTS, u=HALVES)
        nc.vector.memset(x_pairs[:, 1:, TOKENS - SHIFTS + 1 :, :], 0.0)
        x_flipped = flip.tile([P, SLABS_PER_BANK * HALVES, P], F32, name="x_flipped", tag="flipped")
        for u in range(HALVES):
            nc.tensor.transpose(x_flipped[:, u, :], x_rows[:].bitcast(F32)[:, u * P : (u + 1) * P], identity[:])
        nc.vector.tensor_copy(out=x_pairs[:, 0, :, :], in_=x_flipped[:, 0:HALVES, :].rearrange("p u t -> p t u"))
        for s in range(1, SHIFTS):
            nc.vector.tensor_copy(out=x_pairs[:, s, : TOKENS - s, :], in_=x_pairs[:, 0, s:, :])
        nc.vector.quantize_mx(out=x_codes[:].bitcast(FP8X4), scales=x_scales[:], in_=x_grouped[:])

        b_flipped = flip.tile([P, SLABS_PER_BANK * HALVES, P], F32, name="b_flipped", tag="flipped")
        nc.tensor.transpose(b_flipped[:, 0, :], b_rows[:].bitcast(F32), identity[:])
        bias = keep.tile([P, len(WIDTHS) * PARITIES], F32)
        nc.vector.tensor_copy(out=bias[:], in_=b_flipped[:, 0, 0 : len(WIDTHS)].bitcast(BF16))

        n_banks = n_slabs // SLABS_PER_BANK
        w_grouped = []
        w_codes = []
        w_scales = []
        for bank in range(n_banks):
            w_grouped.append(keep.tile([P, SLABS_PER_BANK * SLAB_COLS], BF16, name="w_grouped%d" % bank, align_bytes=64))
            w_codes.append(keep.tile([P, SLABS_PER_BANK * P], U32, name="w_codes%d" % bank, align_bytes=64))
            w_scales.append(keep.tile([P, SLABS_PER_BANK * P], U8, name="w_scales%d" % bank, align_bytes=64))

        def transpose(bank):
            flipped = flip.tile([P, SLABS_PER_BANK * HALVES, P], F32, name="flipped", tag="flipped")
            for t in range(SLABS_PER_BANK * HALVES):
                nc.tensor.transpose(flipped[:, t, :], w_rows[bank][:].bitcast(F32)[:, t * P : (t + 1) * P], identity[:])
            pairs = w_grouped[bank][:].bitcast(F32).rearrange("p (b q u) -> p b q u", b=SLABS_PER_BANK, u=HALVES)
            source = flipped[:].rearrange("p (b u) q -> p b q u", u=HALVES)
            if bank % VECTOR_EMPTIES_EVERY == VECTOR_EMPTIES_EVERY - 1:
                nc.vector.tensor_copy(out=pairs, in_=source)
            else:
                nc.scalar.copy(out=pairs, in_=source)

        def quantise(bank):
            nc.vector.quantize_mx(out=w_codes[bank][:].bitcast(FP8X4), scales=w_scales[bank][:], in_=w_grouped[bank][:])

        code = keep.tile([P, PARITIES, TOKENS], F32)
        nc.vector.memset(code[:], 0.0)

        def by_text(ap, positions):
            return ap.rearrange("q (n p) -> q n p", p=WORDS)[:, :, :positions]

        conv = {}
        for width in WIDTHS:
            conv[width] = sums.tile([P, PARITIES, TOKENS], F32, name="conv%d" % width)

        def convolve(width):
            for j in range(PARITIES):
                for k in range(width):
                    bank, place = divmod(first_slab[width] + j * width + k, SLABS_PER_BANK)
                    slab = slice(place * P, (place + 1) * P)
                    shifted = slice(k * TOKENS, (k + 1) * TOKENS)
                    nc.tensor.matmul_mx(
                        out=conv[width][:, j, :],
                        lhsT=w_codes[bank][:, slab].bitcast(FP8X4),
                        lhsT_scale=w_scales[bank][:, slab],
                        rhs=x_codes[:, shifted].bitcast(FP8X4),
                        rhs_scale=x_scales[:, shifted],
                        start=(k == 0),
                        stop=(k == width - 1),
                    )

        def merge(width):
            positions = WORDS - width + 1
            for j in range(PARITIES):
                column = WIDTHS.index(width) * PARITIES + j
                nc.vector.scalar_tensor_tensor(
                    out=by_text(code[:, j, :], positions),
                    in0=by_text(conv[width][:, j, :], positions),
                    scalar=bias[:, column : column + 1],
                    in1=by_text(code[:, j, :], positions),
                    op0=ALU.add,
                    op1=ALU.max,
                )

        last_bank = {}
        for width in WIDTHS:
            last_bank[(first_slab[width] + PARITIES * width) // SLABS_PER_BANK - 1] = width
        for step in range(n_banks + CONV_LAG + 1):
            if step < n_banks:
                transpose(step)
            if 0 <= step - 1 < n_banks:
                quantise(step - 1)
            if step - CONV_LAG in last_bank:
                convolve(last_bank[step - CONV_LAG])
            if step - CONV_LAG - 1 in last_bank:
                merge(last_bank[step - CONV_LAG - 1])

        squares = keep.tile([P, PARITIES, TOKENS], F32)
        square_sum = sums.tile([P, TOKENS], F32)
        for j in range(PARITIES):
            nc.scalar.activation(out=squares[:, j, :], in_=code[:, j, :], func=ACT.Square)
            nc.tensor.matmul(
                out=square_sum[:], lhsT=ones[:], rhs=squares[:, j, :], start=(j == 0), stop=(j == PARITIES - 1)
            )
        inverse_norm = keep.tile([P, TOKENS], F32)
        nc.scalar.activation(
            out=by_text(inverse_norm[:], POSITIONS), in_=by_text(square_sum[:], POSITIONS), func=ACT.Abs_reciprocal_sqrt
        )
        result = keep.tile([P, TEXTS, PARITIES, POSITIONS], F32)
        for j in range(PARITIES):
            nc.vector.scalar_tensor_tensor(
                out=result[:, :, j, :],
                in0=by_text(inverse_norm[:], POSITIONS),
                scalar=1.0 / EPS,
                in1=by_text(code[:, j, :], POSITIONS),
                op0=ALU.min,
                op1=ALU.mult,
            )
        nc.sync.dma_start(
            out=out.rearrange("n (q j) p -> q n (j p)", j=PARITIES),
            in_=result[:].rearrange("q n j p -> q n (j p)"),
        )
